import numpy as np
import ml_dtypes


def mxq(x, axis, fmt="e4m3"):
    dtype, down = {"e4m3": (ml_dtypes.float8_e4m3fn, 7), "e5m2": (ml_dtypes.float8_e5m2, 14)}[fmt]
    v = np.moveaxis(np.asarray(x, np.float32).astype(ml_dtypes.bfloat16).astype(np.float64), axis, -1)
    blocks = v.reshape(v.shape[:-1] + (-1, 32))
    amax = np.abs(blocks).max(-1, keepdims=True)
    byte = np.maximum(np.where(amax > 0, np.frexp(amax)[1] - 1 + 127, 0) - down, 1)
    scale = np.exp2(byte - 127.0)
    codes = (blocks / scale).astype(np.float32).astype(dtype).astype(np.float64)
    return np.moveaxis((codes * scale).reshape(v.shape), -1, axis)


WIDE = False


def mx_kscale(k):
    if not WIDE:
        return np.ones(k)
    levels = np.array([10, -10, 5, -5, 0])
    a = np.random.permutation(np.resize(levels, k // 512 * 4)).reshape(k // 512, 4)
    idx = np.arange(k)
    return np.exp2(a[idx // 512, idx % 128 // 32])


BF16 = ml_dtypes.bfloat16


def bf(x):
    return np.asarray(x, np.float32).astype(BF16)


def f64(x):
    return np.asarray(x).astype(np.float64)


B, S, D_IN, D_OUT = 2, 256, 1024, 512
THRESHOLD = 0.5


def ternarize(w, threshold=THRESHOLD):
    mag = np.abs(w)
    mask = mag > threshold
    cnt = np.sum(mask)
    ssum = np.sum(np.where(mask, mag, 0.0))
    scale = np.where(cnt > 0, ssum / np.maximum(cnt, 1).astype(np.float64), 1.0)
    ternary = np.sign(w) * mask.astype(np.float64)
    return ternary * scale


def setup_inputs():
    s = mx_kscale(D_IN)
    t = np.maximum(s, 1.0) ** 2
    return {"x": bf(np.random.standard_normal((B, S, D_IN)) * 2.0 / np.sqrt(D_IN) * t),
            "weight": bf(np.random.standard_normal((D_OUT, D_IN)) / t),
            "bias": bf(np.random.standard_normal(D_OUT) * 0.3)}


def reference(x, weight, bias):
    w_t = ternarize(f64(weight))
    return (mxq(f64(x), 2, "e4m3") @ mxq(w_t, 1, "e4m3").T) + f64(bias)

@@ -1,0 +1,184 @@
+from contextlib import ExitStack
+
+import concourse.mybir as mybir
+from concourse.masks import make_identity
+
+F32 = mybir.dt.float32
+BF16 = mybir.dt.bfloat16
+U32 = mybir.dt.uint32
+U8 = mybir.dt.uint8
+FP8X4 = mybir.dt.float8_e4m3fn_x4
+ALU = mybir.AluOpType
+ACT = mybir.ActivationFunctionType
+AXIS = mybir.AxisListType
+
+P = 128
+TOKENS = 512
+D_IN = 1024
+D_OUT = 512
+PACK = 4
+K_PASS = P * PACK
+PASSES = D_IN // K_PASS
+HALVES = 2
+ROW_TILES = 4
+K_BLOCKS = D_IN // P
+LAG = 2
+ROUND_TO_INTEGER = 12582912.0
+
+FLOPS = 2 * TOKENS * D_OUT * D_IN
+
+
+def transpose_row_tile(nc, bank, rows, identity):
+    words = rows.bitcast(F32)
+    for g in range(PASSES):
+        for u in range(HALVES):
+            first = (g * HALVES + u) * P
+            nc.tensor.transpose(bank[:, g, u, :], words[:, first : first + P], identity)
+
+
+def tile_ternarylinear_s_kernel(tc, x, weight, bias, out):
+    nc = tc.nc
+    x_rows = x.flatten_outer_dims()
+    out_rows = out.flatten_outer_dims()
+
+    with ExitStack() as stack:
+        stack.enter_context(tc.manual_schedule())
+        keep = stack.enter_context(tc.tile_pool(name="keep", bufs=1))
+        results = stack.enter_context(tc.tile_pool(name="results", bufs=ROW_TILES))
+        psum_s = stack.enter_context(tc.psum_pool(name="psum_s", bufs=1))
+        psum = stack.enter_context(tc.psum_pool(name="psum", bufs=5))
+
+        w_sb = keep.tile([P, ROW_TILES, D_IN], BF16)
+        x_sb = keep.tile([P, ROW_TILES, D_IN], BF16)
+        bias_all = keep.tile([P, D_OUT], BF16)
+        for j in range(ROW_TILES):
+            nc.sync.dma_start(out=w_sb[:, j, :], in_=weight[j * P : (j + 1) * P, :])
+        for m in range(ROW_TILES):
+            nc.sync.dma_start(out=x_sb[:, m, :], in_=x_rows[m * P : (m + 1) * P, :])
+        nc.sync.dma_start(out=bias_all[:], in_=bias.partition_broadcast(P))
+
+        identity = keep.tile([P, P], F32)
+        make_identity(nc, identity[:])
+        ones = keep.tile([P, P], F32)
+        nc.vector.memset(ones[:], 1.0)
+        two_ones = keep.tile([P, 2], BF16)
+        nc.vector.memset(two_ones[:], 1.0)
+        count_parts = keep.tile([P, ROW_TILES], F32)
+
+        clipped = keep.tile([P, ROW_TILES, D_IN], BF16)
+        ternary = keep.tile([P, ROW_TILES, D_IN], BF16)
+        kept_mag = keep.tile([P, ROW_TILES, D_IN], BF16)
+        kept_one = keep.tile([P, ROW_TILES, D_IN], BF16)
+        ternary_banks = []
+        for j in range(ROW_TILES):
+            nc.vector.tensor_scalar(
+                out=clipped[:, j, :], in0=w_sb[:, j, :],
+                scalar1=-1.0, scalar2=1.0, op0=ALU.max, op1=ALU.min,
+            )
+            nc.vector.tensor_scalar(
+                out=ternary[:, j, :], in0=clipped[:, j, :],
+                scalar1=ROUND_TO_INTEGER, scalar2=ROUND_TO_INTEGER, op0=ALU.add, op1=ALU.subtract,
+            )
+            nc.scalar.activation(
+                out=kept_one[:, j, :], in_=ternary[:, j, :], func=ACT.Square,
+                accum_out=count_parts[:, j : j + 1],
+            )
+            bank = psum.tile([P, PASSES, HALVES, P], F32, name="ternary_bank%d" % j, tag="bank")
+            transpose_row_tile(nc, bank, ternary[:, j, :], identity[:])
+            ternary_banks.append(bank)
+        for j in range(ROW_TILES):
+            nc.vector.tensor_tensor(
+                out=kept_mag[:, j, :], in0=ternary[:, j, :], in1=w_sb[:, j, :], op=ALU.mult
+            )
+        column_sums = psum_s.tile([P, 2], F32)
+        for j in range(ROW_TILES):
+            for c in range(K_BLOCKS):
+                nc.tensor.matmul(
+                    column_sums[:], lhsT=kept_mag[:, j, c * P : (c + 1) * P], rhs=two_ones[:],
+                    start=(j == 0 and c == 0), stop=(j == ROW_TILES - 1 and c == K_BLOCKS - 1),
+                )
+
+        ternary_t = keep.tile([P, PASSES, D_OUT, HALVES], F32)
+
+        def empty_ternary_bank(j):
+            copy_out = nc.scalar.copy if j % 2 == 0 else nc.vector.tensor_copy
+            copy_out(
+                out=ternary_t[:, :, j * P : (j + 1) * P, :],
+                in_=ternary_banks[j][:].rearrange("p g u r -> p g r u"),
+            )
+
+        count_totals = psum_s.tile([P, ROW_TILES], F32)
+        sum_totals = psum_s.tile([P, 2], F32)
+        sum_parts = keep.tile([P, 2], F32)
+        count = keep.tile([P, 1], F32)
+        count_floor = keep.tile([P, 1], F32)
+        inv_count = keep.tile([P, 1], F32)
+        kept_sum = keep.tile([P, 1], F32)
+        nc.tensor.matmul(count_totals[:], lhsT=ones[:], rhs=count_parts[:], start=True, stop=True)
+        empty_ternary_bank(0)
+        empty_ternary_bank(1)
+        nc.vector.tensor_copy(out=sum_parts[:], in_=column_sums[:])
+        nc.tensor.matmul(sum_totals[:], lhsT=ones[:], rhs=sum_parts[:], start=True, stop=True)
+        empty_ternary_bank(2)
+        empty_ternary_bank(3)
+        nc.vector.tensor_reduce(out=count[:], in_=count_totals[:], axis=AXIS.X, op=ALU.add)
+        nc.vector.tensor_scalar(
+            out=count_floor[:], in0=count[:], scalar1=1.0, scalar2=None, op0=ALU.max
+        )
+        nc.vector.tensor_copy(out=kept_sum[:], in_=sum_totals[:, 0:1])
+        nc.vector.reciprocal(out=inv_count[:], in_=count_floor[:])
+
+        x_grouped = keep.tile([P, ROW_TILES, PASSES, P, HALVES], F32, align_bytes=64)
+        for m in range(ROW_TILES):
+            bank = psum.tile([P, PASSES, HALVES, P], F32, name="x_bank%d" % m, tag="bank")
+            transpose_row_tile(nc, bank, x_sb[:, m, :], identity[:])
+            nc.scalar.copy(
+                out=x_grouped[:, m, :, :, :], in_=bank[:].rearrange("p g u r -> p g r u")
+            )
+
+        w_t = keep.tile([P, PASSES, D_OUT * PACK], BF16, align_bytes=64)
+        w_codes = keep.tile([P, PASSES, D_OUT], U32, align_bytes=64)
+        w_scales = keep.tile([P, PASSES, D_OUT], U8, align_bytes=64)
+        for g in range(PASSES):
+            nc.vector.tensor_scalar(
+                out=w_t[:, g, :],
+                in0=ternary_t[:, g, :, :].rearrange("p o u -> p (o u)").bitcast(BF16),
+                scalar1=kept_sum[:, 0:1], scalar2=inv_count[:, 0:1], op0=ALU.mult, op1=ALU.mult,
+            )
+        for g in range(PASSES):
+            nc.vector.quantize_mx(
+                out=w_codes[:, g, :].bitcast(FP8X4), scales=w_scales[:, g, :], in_=w_t[:, g, :]
+            )
+
+        x_codes = keep.tile([P, ROW_TILES, PASSES, P], U32, align_bytes=64)
+        x_scales = keep.tile([P, ROW_TILES, PASSES, P], U8, align_bytes=64)
+
+        def quantise_x(m):
+            nc.vector.quantize_mx(
+                out=x_codes[:, m, :, :].rearrange("p g r -> p (g r)").bitcast(FP8X4),
+                scales=x_scales[:, m, :, :].rearrange("p g r -> p (g r)"),
+                in_=x_grouped[:, m, :, :, :].rearrange("p g r u -> p (g r u)").bitcast(BF16),
+            )
+
+        def multiply_and_store(m):
+            acc = psum.tile([P, D_OUT], F32, name="acc%d" % m, tag="bank")
+            for g in range(PASSES):
+                nc.tensor.matmul_mx(
+                    out=acc[:],
+                    lhsT=x_codes[:, m, g, :].bitcast(FP8X4),
+                    lhsT_scale=x_scales[:, m, g, :],
+                    rhs=w_codes[:, g, :].bitcast(FP8X4),
+                    rhs_scale=w_scales[:, g, :],
+                    start=(g == 0),
+                    stop=(g == PASSES - 1),
+                )
+            result = results.tile([P, D_OUT], F32)
+            nc.vector.tensor_tensor(out=result[:], in0=acc[:], in1=bias_all[:], op=ALU.add)
+            nc.sync.dma_start(out=out_rows[m * P : (m + 1) * P, :], in_=result[:])
+
+        for m in range(ROW_TILES):
+            quantise_x(m)
+            if m >= LAG:
+                multiply_and_store(m - LAG)
+        for m in range(ROW_TILES - LAG, ROW_TILES):
+            multiply_and_store(m)

@@ -22,18 +22,15 @@ PASSES = D_IN // K_PASS
 HALVES = 2
 ROW_TILES = 4
 K_BLOCKS = D_IN // P
-LAG = 2
+SUM_PART = 0
+PARTS = ROW_TILES + 3
+NO_COUNT = 2.0**-60
+WARM_UP = 8
+PAIRS = ROW_TILES // 2
+PAIR_ROWS = 2 * P
 ROUND_TO_INTEGER = 12582912.0
 
 FLOPS = 2 * TOKENS * D_OUT * D_IN
-
-
-def transpose_row_tile(nc, bank, rows, identity):
-    words = rows.bitcast(F32)
-    for g in range(PASSES):
-        for u in range(HALVES):
-            first = (g * HALVES + u) * P
-            nc.tensor.transpose(bank[:, g, u, :], words[:, first : first + P], identity)
 
 
 def tile_ternarylinear_s_kernel(tc, x, weight, bias, out):
@@ -46,15 +43,19 @@ def tile_ternarylinear_s_kernel(tc, x, weight, bias, out):
         keep = stack.enter_context(tc.tile_pool(name="keep", bufs=1))
         results = stack.enter_context(tc.tile_pool(name="results", bufs=ROW_TILES))
         psum_s = stack.enter_context(tc.psum_pool(name="psum_s", bufs=1))
-        psum = stack.enter_context(tc.psum_pool(name="psum", bufs=5))
+        psum_x = stack.enter_context(tc.psum_pool(name="psum_x", bufs=3))
+        psum_w = stack.enter_context(tc.psum_pool(name="psum_w", bufs=ROW_TILES))
 
         w_sb = keep.tile([P, ROW_TILES, D_IN], BF16)
         x_sb = keep.tile([P, ROW_TILES, D_IN], BF16)
         bias_all = keep.tile([P, D_OUT], BF16)
-        for j in range(ROW_TILES):
+        half = D_IN // 2
+        for c in (0, half):
+            nc.sync.dma_start(out=w_sb[:, 0, c : c + half], in_=weight[0:P, c : c + half])
+        for j in range(1, ROW_TILES):
             nc.sync.dma_start(out=w_sb[:, j, :], in_=weight[j * P : (j + 1) * P, :])
-        for m in range(ROW_TILES):
-            nc.sync.dma_start(out=x_sb[:, m, :], in_=x_rows[m * P : (m + 1) * P, :])
+            nc.sync.dma_start(out=x_sb[:, j - 1, :], in_=x_rows[(j - 1) * P : j * P, :])
+        nc.sync.dma_start(out=x_sb[:, ROW_TILES - 1, :], in_=x_rows[(ROW_TILES - 1) * P :, :])
         nc.sync.dma_start(out=bias_all[:], in_=bias.partition_broadcast(P))
 
         identity = keep.tile([P, P], F32)
@@ -63,95 +64,84 @@ def tile_ternarylinear_s_kernel(tc, x, weight, bias, out):
         nc.vector.memset(ones[:], 1.0)
         two_ones = keep.tile([P, 2], BF16)
         nc.vector.memset(two_ones[:], 1.0)
-        count_parts = keep.tile([P, ROW_TILES], F32)
+        parts = keep.tile([P, PARTS], F32)
+        nc.vector.memset(parts[:, PARTS - 1 : PARTS], NO_COUNT)
 
         clipped = keep.tile([P, ROW_TILES, D_IN], BF16)
         ternary = keep.tile([P, ROW_TILES, D_IN], BF16)
         kept_mag = keep.tile([P, ROW_TILES, D_IN], BF16)
         kept_one = keep.tile([P, ROW_TILES, D_IN], BF16)
         ternary_banks = []
-        for j in range(ROW_TILES):
+        for g in range(PASSES):
+            ternary_banks.append([])
+            for h in range(PAIRS):
+                bank = psum_w.tile([P, HALVES, PAIR_ROWS], F32, name="ternary_%d_%d" % (g, h), tag="bank")
+                ternary_banks[g].append(bank)
+
+        def clip(j, c0, c1):
             nc.vector.tensor_scalar(
-                out=clipped[:, j, :], in0=w_sb[:, j, :],
+                out=clipped[:, j, c0:c1], in0=w_sb[:, j, c0:c1],
                 scalar1=-1.0, scalar2=1.0, op0=ALU.max, op1=ALU.min,
             )
+
+        def round_clipped(j, c0, c1):
             nc.vector.tensor_scalar(
-                out=ternary[:, j, :], in0=clipped[:, j, :],
+                out=ternary[:, j, c0:c1], in0=clipped[:, j, c0:c1],
                 scalar1=ROUND_TO_INTEGER, scalar2=ROUND_TO_INTEGER, op0=ALU.add, op1=ALU.subtract,
             )
+
+        def count_kept(j, c0, c1, part):
             nc.scalar.activation(
-                out=kept_one[:, j, :], in_=ternary[:, j, :], func=ACT.Square,
-                accum_out=count_parts[:, j : j + 1],
+                out=kept_one[:, j, c0:c1], in_=ternary[:, j, c0:c1], func=ACT.Square,
+                accum_out=parts[:, part : part + 1],
             )
-            bank = psum.tile([P, PASSES, HALVES, P], F32, name="ternary_bank%d" % j, tag="bank")
-            transpose_row_tile(nc, bank, ternary[:, j, :], identity[:])
-            ternary_banks.append(bank)
-        for j in range(ROW_TILES):
+
+        def transpose_ternary(j):
+            h, i = divmod(j, 2)
+            words = ternary[:, j, :].bitcast(F32)
+            for g in range(PASSES):
+                for u in range(HALVES):
+                    first = (g * HALVES + u) * P
+                    nc.tensor.transpose(
+                        ternary_banks[g][h][:, u, i * P : (i + 1) * P],
+                        words[:, first : first + P],
+                        identity[:],
+                    )
+
+        sums_bank = psum_s.tile([P, 512], F32)
+        column_sums = sums_bank[:, 0:2]
+        totals = sums_bank[:, 16 : 16 + PARTS]
+
+        def keep_magnitudes(j, c0, c1):
             nc.vector.tensor_tensor(
-                out=kept_mag[:, j, :], in0=ternary[:, j, :], in1=w_sb[:, j, :], op=ALU.mult
+                out=kept_mag[:, j, c0:c1], in0=ternary[:, j, c0:c1], in1=w_sb[:, j, c0:c1], op=ALU.mult
             )
-        column_sums = psum_s.tile([P, 2], F32)
-        for j in range(ROW_TILES):
+
+        def add_up_magnitudes(j):
             for c in range(K_BLOCKS):
                 nc.tensor.matmul(
-                    column_sums[:], lhsT=kept_mag[:, j, c * P : (c + 1) * P], rhs=two_ones[:],
+                    column_sums, lhsT=kept_mag[:, j, c * P : (c + 1) * P], rhs=two_ones[:],
                     start=(j == 0 and c == 0), stop=(j == ROW_TILES - 1 and c == K_BLOCKS - 1),
                 )
 
-        ternary_t = keep.tile([P, PASSES, D_OUT, HALVES], F32)
-
-        def empty_ternary_bank(j):
-            copy_out = nc.scalar.copy if j % 2 == 0 else nc.vector.tensor_copy
-            copy_out(
-                out=ternary_t[:, :, j * P : (j + 1) * P, :],
-                in_=ternary_banks[j][:].rearrange("p g u r -> p g r u"),
-            )
-
-        count_totals = psum_s.tile([P, ROW_TILES], F32)
-        sum_totals = psum_s.tile([P, 2], F32)
-        sum_parts = keep.tile([P, 2], F32)
-        count = keep.tile([P, 1], F32)
-        count_floor = keep.tile([P, 1], F32)
-        inv_count = keep.tile([P, 1], F32)
-        kept_sum = keep.tile([P, 1], F32)
-        nc.tensor.matmul(count_totals[:], lhsT=ones[:], rhs=count_parts[:], start=True, stop=True)
-        empty_ternary_bank(0)
-        empty_ternary_bank(1)
-        nc.vector.tensor_copy(out=sum_parts[:], in_=column_sums[:])
-        nc.tensor.matmul(sum_totals[:], lhsT=ones[:], rhs=sum_parts[:], start=True, stop=True)
-        empty_ternary_bank(2)
-        empty_ternary_bank(3)
-        nc.vector.tensor_reduce(out=count[:], in_=count_totals[:], axis=AXIS.X, op=ALU.add)
-        nc.vector.tensor_scalar(
-            out=count_floor[:], in0=count[:], scalar1=1.0, scalar2=None, op0=ALU.max
-        )
-        nc.vector.tensor_copy(out=kept_sum[:], in_=sum_totals[:, 0:1])
-        nc.vector.reciprocal(out=inv_count[:], in_=count_floor[:])
-
         x_grouped = keep.tile([P, ROW_TILES, PASSES, P, HALVES], F32, align_bytes=64)
-        for m in range(ROW_TILES):
-            bank = psum.tile([P, PASSES, HALVES, P], F32, name="x_bank%d" % m, tag="bank")
-            transpose_row_tile(nc, bank, x_sb[:, m, :], identity[:])
-            nc.scalar.copy(
-                out=x_grouped[:, m, :, :, :], in_=bank[:].rearrange("p g u r -> p g r u")
-            )
-
-        w_t = keep.tile([P, PASSES, D_OUT * PACK], BF16, align_bytes=64)
-        w_codes = keep.tile([P, PASSES, D_OUT], U32, align_bytes=64)
-        w_scales = keep.tile([P, PASSES, D_OUT], U8, align_bytes=64)
-        for g in range(PASSES):
-            nc.vector.tensor_scalar(
-                out=w_t[:, g, :],
-                in0=ternary_t[:, g, :, :].rearrange("p o u -> p (o u)").bitcast(BF16),
-                scalar1=kept_sum[:, 0:1], scalar2=inv_count[:, 0:1], op0=ALU.mult, op1=ALU.mult,
-            )
-        for g in range(PASSES):
-            nc.vector.quantize_mx(
-                out=w_codes[:, g, :].bitcast(FP8X4), scales=w_scales[:, g, :], in_=w_t[:, g, :]
-            )
-
         x_codes = keep.tile([P, ROW_TILES, PASSES, P], U32, align_bytes=64)
         x_scales = keep.tile([P, ROW_TILES, PASSES, P], U8, align_bytes=64)
+        x_banks = []
+
+        def transpose_x(m):
+            bank = psum_x.tile([P, PASSES, HALVES, P], F32, name="x_bank%d" % m, tag="x_bank")
+            words = x_sb[:, m, :].bitcast(F32)
+            for g in range(PASSES):
+                for u in range(HALVES):
+                    first = (g * HALVES + u) * P
+                    nc.tensor.transpose(bank[:, g, u, :], words[:, first : first + P], identity[:])
+            x_banks.append(bank)
+
+        def empty_x_bank(m, copy_out):
+            copy_out(
+                out=x_grouped[:, m, :, :, :], in_=x_banks[m][:].rearrange("p g u r -> p g r u")
+            )
 
         def quantise_x(m):
             nc.vector.quantize_mx(
@@ -160,25 +150,113 @@ def tile_ternarylinear_s_kernel(tc, x, weight, bias, out):
                 in_=x_grouped[:, m, :, :, :].rearrange("p g r u -> p (g r u)").bitcast(BF16),
             )
 
-        def multiply_and_store(m):
-            acc = psum.tile([P, D_OUT], F32, name="acc%d" % m, tag="bank")
-            for g in range(PASSES):
-                nc.tensor.matmul_mx(
-                    out=acc[:],
-                    lhsT=x_codes[:, m, g, :].bitcast(FP8X4),
-                    lhsT_scale=x_scales[:, m, g, :],
-                    rhs=w_codes[:, g, :].bitcast(FP8X4),
-                    rhs_scale=w_scales[:, g, :],
-                    start=(g == 0),
-                    stop=(g == PASSES - 1),
-                )
-            result = results.tile([P, D_OUT], F32)
-            nc.vector.tensor_tensor(out=result[:], in0=acc[:], in1=bias_all[:], op=ALU.add)
-            nc.sync.dma_start(out=out_rows[m * P : (m + 1) * P, :], in_=result[:])
+        clip(0, 0, half)
+        clip(0, half, D_IN)
+        round_clipped(0, 0, half)
+        count_kept(0, 0, half, 1)
+        round_clipped(0, half, D_IN)
+        count_kept(0, half, D_IN, 2)
+        transpose_ternary(0)
+        for j in range(1, ROW_TILES):
+            clip(j, 0, D_IN)
+            keep_magnitudes(j - 1, 0, D_IN)
+            if j < ROW_TILES - 1:
+                round_clipped(j, 0, D_IN)
+            else:
+                round_clipped(j, 0, half)
+                round_clipped(j, half, D_IN)
+            count_kept(j, 0, D_IN, j + 2)
+            transpose_x(j - 1)
+            transpose_ternary(j)
+            add_up_magnitudes(j - 1)
+        keep_magnitudes(ROW_TILES - 1, 0, half)
+        keep_magnitudes(ROW_TILES - 1, half, D_IN)
+        add_up_magnitudes(ROW_TILES - 1)
+        empty_x_bank(0, nc.vector.tensor_copy)
 
+        count = keep.tile([P, 1], F32)
+        inv_count = keep.tile([P, 1], F32)
+        scale = keep.tile([P, 1], F32)
+        empty_x_bank(1, nc.scalar.copy)
+        empty_x_bank(2, nc.scalar.copy)
+        nc.vector.tensor_copy(
+            out=parts[:, SUM_PART : SUM_PART + 1], in_=column_sums[:, 0:1]
+        )
+        quantise_x(0)
+        nc.tensor.matmul(totals, lhsT=ones[:], rhs=parts[:], start=True, stop=True)
+        transpose_x(3)
+        nc.vector.tensor_reduce(
+            out=count[:], in_=totals[:, SUM_PART + 1 :], axis=AXIS.X, op=ALU.add
+        )
+        quantise_x(1)
+        nc.vector.reciprocal(out=inv_count[:], in_=count[:])
+        nc.vector.tensor_scalar(
+            out=scale[:], in0=totals[:, SUM_PART : SUM_PART + 1], scalar1=inv_count[:, 0:1], scalar2=None, op0=ALU.mult
+        )
+
+        warm = psum_x.tile([P, PASSES, HALVES, P], F32, name="warm", tag="x_bank")
+        for i in range(WARM_UP):
+            nc.tensor.matmul(warm[:, 0, 0, :], lhsT=ones[:], rhs=identity[:], start=True, stop=True)
+
+        w_t = keep.tile([P, PASSES, D_OUT * PACK], BF16, align_bytes=64)
+        w_codes = keep.tile([P, PASSES, D_OUT], U32, align_bytes=64)
+        w_scales = keep.tile([P, PASSES, D_OUT], U8, align_bytes=64)
+
+        def w_t_operands(g, h):
+            out = w_t[:, g, h * PAIR_ROWS * PACK : (h + 1) * PAIR_ROWS * PACK]
+            values = ternary_banks[g][h][:].rearrange("p u r -> p (u r)").bitcast(BF16)
+            return (
+                out.rearrange("p (r u e) -> p r u e", u=HALVES, e=2),
+                values.rearrange("p (u r e) -> p r u e", u=HALVES, e=2),
+            )
+
+        def quantise_w(g):
+            nc.vector.quantize_mx(
+                out=w_codes[:, g, :].bitcast(FP8X4), scales=w_scales[:, g, :], in_=w_t[:, g, :]
+            )
+
+        def scale_w_on_vector(g, h):
+            w_out, values = w_t_operands(g, h)
+            nc.vector.tensor_scalar(
+                out=w_out, in0=values, scalar1=totals[:, SUM_PART : SUM_PART + 1], scalar2=inv_count[:, 0:1],
+                op0=ALU.mult, op1=ALU.mult,
+            )
+
+        def scale_w_on_scalar(g, h):
+            w_out, values = w_t_operands(g, h)
+            nc.scalar.activation(out=w_out, in_=values, func=ACT.Copy, scale=scale[:, 0:1])
+
+        scale_w_on_scalar(0, 1)
+        scale_w_on_scalar(1, 1)
+        empty_x_bank(3, nc.scalar.copy)
+        scale_w_on_vector(0, 0)
+        scale_w_on_vector(1, 0)
+        quantise_x(2)
+        quantise_w(0)
+        quantise_w(1)
+        quantise_x(ROW_TILES - 1)
+
+        accs = []
         for m in range(ROW_TILES):
-            quantise_x(m)
-            if m >= LAG:
-                multiply_and_store(m - LAG)
-        for m in range(ROW_TILES - LAG, ROW_TILES):
-            multiply_and_store(m)
+            accs.append(psum_w.tile([P, D_OUT], F32, name="acc%d" % m, tag="bank"))
+
+        def multiply(m, g):
+            nc.tensor.matmul_mx(
+                out=accs[m][:],
+                lhsT=x_codes[:, m, g, :].bitcast(FP8X4),
+                lhsT_scale=x_scales[:, m, g, :],
+                rhs=w_codes[:, g, :].bitcast(FP8X4),
+                rhs_scale=w_scales[:, g, :],
+                start=(g == 0),
+                stop=(g == PASSES - 1),
+            )
+
+        for m in range(ROW_TILES - 1):
+            multiply(m, 0)
+        for m in range(ROW_TILES):
+            if m == ROW_TILES - 1:
+                multiply(m, 0)
+            multiply(m, 1)
+            result = results.tile([P, D_OUT], F32)
+            nc.vector.tensor_tensor(out=result[:], in0=accs[m][:], in1=bias_all[:], op=ALU.add)
+            nc.sync.dma_start(out=out_rows[m * P : (m + 1) * P, :], in_=result[:])

@@ -25,7 +25,7 @@ K_BLOCKS = D_IN // P
 SUM_PART = 0
 PARTS = ROW_TILES + 3
 NO_COUNT = 2.0**-60
-WARM_UP = 8
+WARM_START, WARM_END = 4, 8
 PAIRS = ROW_TILES // 2
 PAIR_ROWS = 2 * P
 ROUND_TO_INTEGER = 12582912.0
@@ -150,6 +150,12 @@ def tile_ternarylinear_s_kernel(tc, x, weight, bias, out):
                 in_=x_grouped[:, m, :, :, :].rearrange("p g r u -> p (g r u)").bitcast(BF16),
             )
 
+        def warm_up(n):
+            bank = psum_x.tile([P, PASSES, HALVES, P], F32, name="warm", tag="x_bank")
+            for i in range(n):
+                nc.tensor.matmul(bank[:, 0, 0, :], lhsT=ones[:], rhs=ones[:], start=True, stop=True)
+
+        warm_up(WARM_START)
         clip(0, 0, half)
         clip(0, half, D_IN)
         round_clipped(0, 0, half)
@@ -167,7 +173,8 @@ def tile_ternarylinear_s_kernel(tc, x, weight, bias, out):
                 round_clipped(j, half, D_IN)
             count_kept(j, 0, D_IN, j + 2)
             transpose_x(j - 1)
-            transpose_ternary(j)
+            if j < ROW_TILES - 1:
+                transpose_ternary(j)
             add_up_magnitudes(j - 1)
         keep_magnitudes(ROW_TILES - 1, 0, half)
         keep_magnitudes(ROW_TILES - 1, half, D_IN)
@@ -184,6 +191,7 @@ def tile_ternarylinear_s_kernel(tc, x, weight, bias, out):
         )
         quantise_x(0)
         nc.tensor.matmul(totals, lhsT=ones[:], rhs=parts[:], start=True, stop=True)
+        transpose_ternary(ROW_TILES - 1)
         transpose_x(3)
         nc.vector.tensor_reduce(
             out=count[:], in_=totals[:, SUM_PART + 1 :], axis=AXIS.X, op=ALU.add
@@ -194,9 +202,7 @@ def tile_ternarylinear_s_kernel(tc, x, weight, bias, out):
             out=scale[:], in0=totals[:, SUM_PART : SUM_PART + 1], scalar1=inv_count[:, 0:1], scalar2=None, op0=ALU.mult
         )
 
-        warm = psum_x.tile([P, PASSES, HALVES, P], F32, name="warm", tag="x_bank")
-        for i in range(WARM_UP):
-            nc.tensor.matmul(warm[:, 0, 0, :], lhsT=ones[:], rhs=identity[:], start=True, stop=True)
+        warm_up(WARM_END)
 
         w_t = keep.tile([P, PASSES, D_OUT * PACK], BF16, align_bytes=64)
         w_codes = keep.tile([P, PASSES, D_OUT], U32, align_bytes=64)

@@ -22,10 +22,9 @@ PASSES = D_IN // K_PASS
 HALVES = 2
 ROW_TILES = 4
 K_BLOCKS = D_IN // P
-SUM_PART = 0
-PARTS = ROW_TILES + 3
+COUNT_PARTS = ROW_TILES + 3
 NO_COUNT = 2.0**-60
-WARM_START, WARM_END = 4, 8
+WARM_START, WARM_END = 4, 3
 PAIRS = ROW_TILES // 2
 PAIR_ROWS = 2 * P
 ROUND_TO_INTEGER = 12582912.0
@@ -43,7 +42,7 @@ def tile_ternarylinear_s_kernel(tc, x, weight, bias, out):
         keep = stack.enter_context(tc.tile_pool(name="keep", bufs=1))
         results = stack.enter_context(tc.tile_pool(name="results", bufs=ROW_TILES))
         psum_s = stack.enter_context(tc.psum_pool(name="psum_s", bufs=1))
-        psum_x = stack.enter_context(tc.psum_pool(name="psum_x", bufs=3))
+        psum_x = stack.enter_context(tc.psum_pool(name="psum_x", bufs=2))
         psum_w = stack.enter_context(tc.psum_pool(name="psum_w", bufs=ROW_TILES))
 
         w_sb = keep.tile([P, ROW_TILES, D_IN], BF16)
@@ -54,8 +53,10 @@ def tile_ternarylinear_s_kernel(tc, x, weight, bias, out):
             nc.sync.dma_start(out=w_sb[:, 0, c : c + half], in_=weight[0:P, c : c + half])
         for j in range(1, ROW_TILES):
             nc.sync.dma_start(out=w_sb[:, j, :], in_=weight[j * P : (j + 1) * P, :])
-            nc.sync.dma_start(out=x_sb[:, j - 1, :], in_=x_rows[(j - 1) * P : j * P, :])
-        nc.sync.dma_start(out=x_sb[:, ROW_TILES - 1, :], in_=x_rows[(ROW_TILES - 1) * P :, :])
+            if j == 1:
+                nc.sync.dma_start(out=x_sb[:, 0, :], in_=x_rows[0:P, :])
+        for m in range(1, ROW_TILES):
+            nc.sync.dma_start(out=x_sb[:, m, :], in_=x_rows[m * P : (m + 1) * P, :])
         nc.sync.dma_start(out=bias_all[:], in_=bias.partition_broadcast(P))
 
         identity = keep.tile([P, P], F32)
@@ -64,8 +65,8 @@ def tile_ternarylinear_s_kernel(tc, x, weight, bias, out):
         nc.vector.memset(ones[:], 1.0)
         two_ones = keep.tile([P, 2], BF16)
         nc.vector.memset(two_ones[:], 1.0)
-        parts = keep.tile([P, PARTS], F32)
-        nc.vector.memset(parts[:, PARTS - 1 : PARTS], NO_COUNT)
+        count_parts = keep.tile([P, COUNT_PARTS], F32)
+        nc.vector.memset(count_parts[:, COUNT_PARTS - 1 : COUNT_PARTS], NO_COUNT)
 
         clipped = keep.tile([P, ROW_TILES, D_IN], BF16)
         ternary = keep.tile([P, ROW_TILES, D_IN], BF16)
@@ -93,7 +94,14 @@ def tile_ternarylinear_s_kernel(tc, x, weight, bias, out):
         def count_kept(j, c0, c1, part):
             nc.scalar.activation(
                 out=kept_one[:, j, c0:c1], in_=ternary[:, j, c0:c1], func=ACT.Square,
-                accum_out=parts[:, part : part + 1],
+                accum_out=count_parts[:, part : part + 1],
+            )
+
+        def count_kept_on_vector(j, c0, c1, part):
+            nc.vector.tensor_scalar(
+                out=kept_one[:, j, c0:c1], in0=ternary[:, j, c0:c1],
+                scalar1=0.0, scalar2=None, op0=ALU.not_equal, op1=ALU.add,
+                accum_out=count_parts[:, part : part + 1],
             )
 
         def transpose_ternary(j):
@@ -108,9 +116,12 @@ def tile_ternarylinear_s_kernel(tc, x, weight, bias, out):
                         identity[:],
                     )
 
-        sums_bank = psum_s.tile([P, 512], F32)
-        column_sums = sums_bank[:, 0:2]
-        totals = sums_bank[:, 16 : 16 + PARTS]
+        sum_bank = psum_s.tile([P, 512], F32)
+        column_sums = sum_bank[:, 0:2]
+        sum_total = sum_bank[:, 16:18]
+        count_bank = psum_s.tile([P, 512], F32)
+        count_totals = count_bank[:, 0:COUNT_PARTS]
+        warm_columns = count_bank[:, P : 2 * P]
 
         def keep_magnitudes(j, c0, c1):
             nc.vector.tensor_tensor(
@@ -151,17 +162,16 @@ def tile_ternarylinear_s_kernel(tc, x, weight, bias, out):
             )
 
         def warm_up(n):
-            bank = psum_x.tile([P, PASSES, HALVES, P], F32, name="warm", tag="x_bank")
             for i in range(n):
-                nc.tensor.matmul(bank[:, 0, 0, :], lhsT=ones[:], rhs=ones[:], start=True, stop=True)
+                nc.tensor.matmul(warm_columns, lhsT=ones[:], rhs=ones[:], start=True, stop=True)
 
         warm_up(WARM_START)
         clip(0, 0, half)
         clip(0, half, D_IN)
         round_clipped(0, 0, half)
-        count_kept(0, 0, half, 1)
+        count_kept(0, 0, half, 0)
         round_clipped(0, half, D_IN)
-        count_kept(0, half, D_IN, 2)
+        count_kept(0, half, D_IN, 1)
         transpose_ternary(0)
         for j in range(1, ROW_TILES):
             clip(j, 0, D_IN)
@@ -171,76 +181,75 @@ def tile_ternarylinear_s_kernel(tc, x, weight, bias, out):
             else:
                 round_clipped(j, 0, half)
                 round_clipped(j, half, D_IN)
-            count_kept(j, 0, D_IN, j + 2)
-            transpose_x(j - 1)
+            count_kept(j, 0, D_IN if j < ROW_TILES - 1 else half, j + 1)
             if j < ROW_TILES - 1:
+                transpose_x(j - 1)
                 transpose_ternary(j)
             add_up_magnitudes(j - 1)
         keep_magnitudes(ROW_TILES - 1, 0, half)
         keep_magnitudes(ROW_TILES - 1, half, D_IN)
+        count_kept_on_vector(ROW_TILES - 1, half, D_IN, ROW_TILES + 1)
         add_up_magnitudes(ROW_TILES - 1)
-        empty_x_bank(0, nc.vector.tensor_copy)
 
+        sum_parts = keep.tile([P, 2], F32)
         count = keep.tile([P, 1], F32)
         inv_count = keep.tile([P, 1], F32)
         scale = keep.tile([P, 1], F32)
+        empty_x_bank(0, nc.scalar.copy)
         empty_x_bank(1, nc.scalar.copy)
-        empty_x_bank(2, nc.scalar.copy)
-        nc.vector.tensor_copy(
-            out=parts[:, SUM_PART : SUM_PART + 1], in_=column_sums[:, 0:1]
-        )
+        nc.vector.tensor_copy(out=sum_parts[:], in_=column_sums)
+        nc.tensor.matmul(count_totals, lhsT=ones[:], rhs=count_parts[:], start=True, stop=True)
+        nc.tensor.matmul(sum_total, lhsT=ones[:], rhs=sum_parts[:], start=True, stop=True)
+        nc.vector.tensor_reduce(out=count[:], in_=count_totals, axis=AXIS.X, op=ALU.add)
         quantise_x(0)
-        nc.tensor.matmul(totals, lhsT=ones[:], rhs=parts[:], start=True, stop=True)
-        transpose_ternary(ROW_TILES - 1)
-        transpose_x(3)
-        nc.vector.tensor_reduce(
-            out=count[:], in_=totals[:, SUM_PART + 1 :], axis=AXIS.X, op=ALU.add
-        )
-        quantise_x(1)
         nc.vector.reciprocal(out=inv_count[:], in_=count[:])
+        quantise_x(1)
         nc.vector.tensor_scalar(
-            out=scale[:], in0=totals[:, SUM_PART : SUM_PART + 1], scalar1=inv_count[:, 0:1], scalar2=None, op0=ALU.mult
+            out=scale[:], in0=sum_total[:, 0:1], scalar1=inv_count[:, 0:1], scalar2=None, op0=ALU.mult
         )
-
+        transpose_ternary(ROW_TILES - 1)
+        transpose_x(2)
+        transpose_x(3)
         warm_up(WARM_END)
 
         w_t = keep.tile([P, PASSES, D_OUT * PACK], BF16, align_bytes=64)
         w_codes = keep.tile([P, PASSES, D_OUT], U32, align_bytes=64)
         w_scales = keep.tile([P, PASSES, D_OUT], U8, align_bytes=64)
 
-        def w_t_operands(g, h):
-            out = w_t[:, g, h * PAIR_ROWS * PACK : (h + 1) * PAIR_ROWS * PACK]
+        def w_t_operands(g, h, r0, r1):
+            first = h * PAIR_ROWS
+            out = w_t[:, g, (first + r0) * PACK : (first + r1) * PACK]
             values = ternary_banks[g][h][:].rearrange("p u r -> p (u r)").bitcast(BF16)
-            return (
-                out.rearrange("p (r u e) -> p r u e", u=HALVES, e=2),
-                values.rearrange("p (u r e) -> p r u e", u=HALVES, e=2),
-            )
+            values = values.rearrange("p (u r e) -> p r u e", u=HALVES, e=2)
+            return out.rearrange("p (r u e) -> p r u e", u=HALVES, e=2), values[:, r0:r1, :, :]
 
         def quantise_w(g):
             nc.vector.quantize_mx(
                 out=w_codes[:, g, :].bitcast(FP8X4), scales=w_scales[:, g, :], in_=w_t[:, g, :]
             )
 
-        def scale_w_on_vector(g, h):
-            w_out, values = w_t_operands(g, h)
+        def scale_w_on_vector(g, h, r0, r1):
+            w_out, values = w_t_operands(g, h, r0, r1)
             nc.vector.tensor_scalar(
-                out=w_out, in0=values, scalar1=totals[:, SUM_PART : SUM_PART + 1], scalar2=inv_count[:, 0:1],
+                out=w_out, in0=values, scalar1=sum_total[:, 0:1], scalar2=inv_count[:, 0:1],
                 op0=ALU.mult, op1=ALU.mult,
             )
 
-        def scale_w_on_scalar(g, h):
-            w_out, values = w_t_operands(g, h)
+        def scale_w_on_scalar(g, h, r0, r1):
+            w_out, values = w_t_operands(g, h, r0, r1)
             nc.scalar.activation(out=w_out, in_=values, func=ACT.Copy, scale=scale[:, 0:1])
 
-        scale_w_on_scalar(0, 1)
-        scale_w_on_scalar(1, 1)
+        scale_w_on_scalar(0, 1, 0, PAIR_ROWS)
+        scale_w_on_vector(0, 0, 0, PAIR_ROWS)
+        scale_w_on_vector(1, 0, 0, PAIR_ROWS)
+        scale_w_on_vector(1, 1, 0, P)
+        scale_w_on_scalar(1, 1, P, PAIR_ROWS)
+        empty_x_bank(2, nc.scalar.copy)
         empty_x_bank(3, nc.scalar.copy)
-        scale_w_on_vector(0, 0)
-        scale_w_on_vector(1, 0)
-        quantise_x(2)
         quantise_w(0)
         quantise_w(1)
-        quantise_x(ROW_TILES - 1)
+        quantise_x(2)
+        quantise_x(3)
 
         accs = []
         for m in range(ROW_TILES):
@@ -257,10 +266,10 @@ def tile_ternarylinear_s_kernel(tc, x, weight, bias, out):
                 stop=(g == PASSES - 1),
             )
 
-        for m in range(ROW_TILES - 1):
+        for m in range(2):
             multiply(m, 0)
         for m in range(ROW_TILES):
-            if m == ROW_TILES - 1:
+            if m >= 2:
                 multiply(m, 0)
             multiply(m, 1)
             result = results.tile([P, D_OUT], F32)

@@ -174,6 +174,7 @@ def tile_ternarylinear_s_kernel(tc, x, weight, bias, out):
         count_kept(0, half, D_IN, 1)
         transpose_ternary(0)
         for j in range(1, ROW_TILES):
+            warm_up(1)
             clip(j, 0, D_IN)
             keep_magnitudes(j - 1, 0, D_IN)
             if j < ROW_TILES - 1:

from contextlib import ExitStack

import concourse.mybir as mybir
from concourse.masks import make_identity

F32 = mybir.dt.float32
BF16 = mybir.dt.bfloat16
U32 = mybir.dt.uint32
U8 = mybir.dt.uint8
FP8X4 = mybir.dt.float8_e4m3fn_x4
ALU = mybir.AluOpType
ACT = mybir.ActivationFunctionType
AXIS = mybir.AxisListType

P = 128
TOKENS = 512
D_IN = 1024
D_OUT = 512
PACK = 4
K_PASS = P * PACK
PASSES = D_IN // K_PASS
HALVES = 2
ROW_TILES = 4
K_BLOCKS = D_IN // P
COUNT_PARTS = ROW_TILES + 3
NO_COUNT = 2.0**-60
WARM_START, WARM_END = 4, 3
PAIRS = ROW_TILES // 2
PAIR_ROWS = 2 * P
ROUND_TO_INTEGER = 12582912.0

FLOPS = 2 * TOKENS * D_OUT * D_IN


def tile_ternarylinear_s_kernel(tc, x, weight, bias, out):
    nc = tc.nc
    x_rows = x.flatten_outer_dims()
    out_rows = out.flatten_outer_dims()

    with ExitStack() as stack:
        stack.enter_context(tc.manual_schedule())
        keep = stack.enter_context(tc.tile_pool(name="keep", bufs=1))
        results = stack.enter_context(tc.tile_pool(name="results", bufs=ROW_TILES))
        psum_s = stack.enter_context(tc.psum_pool(name="psum_s", bufs=1))
        psum_x = stack.enter_context(tc.psum_pool(name="psum_x", bufs=2))
        psum_w = stack.enter_context(tc.psum_pool(name="psum_w", bufs=ROW_TILES))

        w_sb = keep.tile([P, ROW_TILES, D_IN], BF16)
        x_sb = keep.tile([P, ROW_TILES, D_IN], BF16)
        bias_all = keep.tile([P, D_OUT], BF16)
        half = D_IN // 2
        for c in (0, half):
            nc.sync.dma_start(out=w_sb[:, 0, c : c + half], in_=weight[0:P, c : c + half])
        for j in range(1, ROW_TILES):
            nc.sync.dma_start(out=w_sb[:, j, :], in_=weight[j * P : (j + 1) * P, :])
            if j == 1:
                nc.sync.dma_start(out=x_sb[:, 0, :], in_=x_rows[0:P, :])
        for m in range(1, ROW_TILES):
            nc.sync.dma_start(out=x_sb[:, m, :], in_=x_rows[m * P : (m + 1) * P, :])
        nc.sync.dma_start(out=bias_all[:], in_=bias.partition_broadcast(P))

        identity = keep.tile([P, P], F32)
        make_identity(nc, identity[:])
        ones = keep.tile([P, P], F32)
        nc.vector.memset(ones[:], 1.0)
        two_ones = keep.tile([P, 2], BF16)
        nc.vector.memset(two_ones[:], 1.0)
        count_parts = keep.tile([P, COUNT_PARTS], F32)
        nc.vector.memset(count_parts[:, COUNT_PARTS - 1 : COUNT_PARTS], NO_COUNT)

        clipped = keep.tile([P, ROW_TILES, D_IN], BF16)
        ternary = keep.tile([P, ROW_TILES, D_IN], BF16)
        kept_mag = keep.tile([P, ROW_TILES, D_IN], BF16)
        kept_one = keep.tile([P, ROW_TILES, D_IN], BF16)
        ternary_banks = []
        for g in range(PASSES):
            ternary_banks.append([])
            for h in range(PAIRS):
                bank = psum_w.tile([P, HALVES, PAIR_ROWS], F32, name="ternary_%d_%d" % (g, h), tag="bank")
                ternary_banks[g].append(bank)

        def clip(j, c0, c1):
            nc.vector.tensor_scalar(
                out=clipped[:, j, c0:c1], in0=w_sb[:, j, c0:c1],
                scalar1=-1.0, scalar2=1.0, op0=ALU.max, op1=ALU.min,
            )

        def round_clipped(j, c0, c1):
            nc.vector.tensor_scalar(
                out=ternary[:, j, c0:c1], in0=clipped[:, j, c0:c1],
                scalar1=ROUND_TO_INTEGER, scalar2=ROUND_TO_INTEGER, op0=ALU.add, op1=ALU.subtract,
            )

        def count_kept(j, c0, c1, part):
            nc.scalar.activation(
                out=kept_one[:, j, c0:c1], in_=ternary[:, j, c0:c1], func=ACT.Square,
                accum_out=count_parts[:, part : part + 1],
            )

        def count_kept_on_vector(j, c0, c1, part):
            nc.vector.tensor_scalar(
                out=kept_one[:, j, c0:c1], in0=ternary[:, j, c0:c1],
                scalar1=0.0, scalar2=None, op0=ALU.not_equal, op1=ALU.add,
                accum_out=count_parts[:, part : part + 1],
            )

        def transpose_ternary(j):
            h, i = divmod(j, 2)
            words = ternary[:, j, :].bitcast(F32)
            for g in range(PASSES):
                for u in range(HALVES):
                    first = (g * HALVES + u) * P
                    nc.tensor.transpose(
                        ternary_banks[g][h][:, u, i * P : (i + 1) * P],
                        words[:, first : first + P],
                        identity[:],
                    )

        sum_bank = psum_s.tile([P, 512], F32)
        column_sums = sum_bank[:, 0:2]
        sum_total = sum_bank[:, 16:18]
        count_bank = psum_s.tile([P, 512], F32)
        count_totals = count_bank[:, 0:COUNT_PARTS]
        warm_columns = count_bank[:, P : 2 * P]

        def keep_magnitudes(j, c0, c1):
            nc.vector.tensor_tensor(
                out=kept_mag[:, j, c0:c1], in0=ternary[:, j, c0:c1], in1=w_sb[:, j, c0:c1], op=ALU.mult
            )

        def add_up_magnitudes(j):
            for c in range(K_BLOCKS):
                nc.tensor.matmul(
                    column_sums, lhsT=kept_mag[:, j, c * P : (c + 1) * P], rhs=two_ones[:],
                    start=(j == 0 and c == 0), stop=(j == ROW_TILES - 1 and c == K_BLOCKS - 1),
                )

        x_grouped = keep.tile([P, ROW_TILES, PASSES, P, HALVES], F32, align_bytes=64)
        x_codes = keep.tile([P, ROW_TILES, PASSES, P], U32, align_bytes=64)
        x_scales = keep.tile([P, ROW_TILES, PASSES, P], U8, align_bytes=64)
        x_banks = []

        def transpose_x(m):
            bank = psum_x.tile([P, PASSES, HALVES, P], F32, name="x_bank%d" % m, tag="x_bank")
            words = x_sb[:, m, :].bitcast(F32)
            for g in range(PASSES):
                for u in range(HALVES):
                    first = (g * HALVES + u) * P
                    nc.tensor.transpose(bank[:, g, u, :], words[:, first : first + P], identity[:])
            x_banks.append(bank)

        def empty_x_bank(m, copy_out):
            copy_out(
                out=x_grouped[:, m, :, :, :], in_=x_banks[m][:].rearrange("p g u r -> p g r u")
            )

        def quantise_x(m):
            nc.vector.quantize_mx(
                out=x_codes[:, m, :, :].rearrange("p g r -> p (g r)").bitcast(FP8X4),
                scales=x_scales[:, m, :, :].rearrange("p g r -> p (g r)"),
                in_=x_grouped[:, m, :, :, :].rearrange("p g r u -> p (g r u)").bitcast(BF16),
            )

        def warm_up(n):
            for i in range(n):
                nc.tensor.matmul(warm_columns, lhsT=ones[:], rhs=ones[:], start=True, stop=True)

        warm_up(WARM_START)
        clip(0, 0, half)
        clip(0, half, D_IN)
        round_clipped(0, 0, half)
        count_kept(0, 0, half, 0)
        round_clipped(0, half, D_IN)
        count_kept(0, half, D_IN, 1)
        transpose_ternary(0)
        for j in range(1, ROW_TILES):
            warm_up(1)
            clip(j, 0, D_IN)
            keep_magnitudes(j - 1, 0, D_IN)
            if j < ROW_TILES - 1:
                round_clipped(j, 0, D_IN)
            else:
                round_clipped(j, 0, half)
                round_clipped(j, half, D_IN)
            count_kept(j, 0, D_IN if j < ROW_TILES - 1 else half, j + 1)
            if j < ROW_TILES - 1:
                transpose_x(j - 1)
                transpose_ternary(j)
            add_up_magnitudes(j - 1)
        keep_magnitudes(ROW_TILES - 1, 0, half)
        keep_magnitudes(ROW_TILES - 1, half, D_IN)
        count_kept_on_vector(ROW_TILES - 1, half, D_IN, ROW_TILES + 1)
        add_up_magnitudes(ROW_TILES - 1)

        sum_parts = keep.tile([P, 2], F32)
        count = keep.tile([P, 1], F32)
        inv_count = keep.tile([P, 1], F32)
        scale = keep.tile([P, 1], F32)
        empty_x_bank(0, nc.scalar.copy)
        empty_x_bank(1, nc.scalar.copy)
        nc.vector.tensor_copy(out=sum_parts[:], in_=column_sums)
        nc.tensor.matmul(count_totals, lhsT=ones[:], rhs=count_parts[:], start=True, stop=True)
        nc.tensor.matmul(sum_total, lhsT=ones[:], rhs=sum_parts[:], start=True, stop=True)
        nc.vector.tensor_reduce(out=count[:], in_=count_totals, axis=AXIS.X, op=ALU.add)
        quantise_x(0)
        nc.vector.reciprocal(out=inv_count[:], in_=count[:])
        quantise_x(1)
        nc.vector.tensor_scalar(
            out=scale[:], in0=sum_total[:, 0:1], scalar1=inv_count[:, 0:1], scalar2=None, op0=ALU.mult
        )
        transpose_ternary(ROW_TILES - 1)
        transpose_x(2)
        transpose_x(3)
        warm_up(WARM_END)

        w_t = keep.tile([P, PASSES, D_OUT * PACK], BF16, align_bytes=64)
        w_codes = keep.tile([P, PASSES, D_OUT], U32, align_bytes=64)
        w_scales = keep.tile([P, PASSES, D_OUT], U8, align_bytes=64)

        def w_t_operands(g, h, r0, r1):
            first = h * PAIR_ROWS
            out = w_t[:, g, (first + r0) * PACK : (first + r1) * PACK]
            values = ternary_banks[g][h][:].rearrange("p u r -> p (u r)").bitcast(BF16)
            values = values.rearrange("p (u r e) -> p r u e", u=HALVES, e=2)
            return out.rearrange("p (r u e) -> p r u e", u=HALVES, e=2), values[:, r0:r1, :, :]

        def quantise_w(g):
            nc.vector.quantize_mx(
                out=w_codes[:, g, :].bitcast(FP8X4), scales=w_scales[:, g, :], in_=w_t[:, g, :]
            )

        def scale_w_on_vector(g, h, r0, r1):
            w_out, values = w_t_operands(g, h, r0, r1)
            nc.vector.tensor_scalar(
                out=w_out, in0=values, scalar1=sum_total[:, 0:1], scalar2=inv_count[:, 0:1],
                op0=ALU.mult, op1=ALU.mult,
            )

        def scale_w_on_scalar(g, h, r0, r1):
            w_out, values = w_t_operands(g, h, r0, r1)
            nc.scalar.activation(out=w_out, in_=values, func=ACT.Copy, scale=scale[:, 0:1])

        scale_w_on_scalar(0, 1, 0, PAIR_ROWS)
        scale_w_on_vector(0, 0, 0, PAIR_ROWS)
        scale_w_on_vector(1, 0, 0, PAIR_ROWS)
        scale_w_on_vector(1, 1, 0, P)
        scale_w_on_scalar(1, 1, P, PAIR_ROWS)
        empty_x_bank(2, nc.scalar.copy)
        empty_x_bank(3, nc.scalar.copy)
        quantise_w(0)
        quantise_w(1)
        quantise_x(2)
        quantise_x(3)

        accs = []
        for m in range(ROW_TILES):
            accs.append(psum_w.tile([P, D_OUT], F32, name="acc%d" % m, tag="bank"))

        def multiply(m, g):
            nc.tensor.matmul_mx(
                out=accs[m][:],
                lhsT=x_codes[:, m, g, :].bitcast(FP8X4),
                lhsT_scale=x_scales[:, m, g, :],
                rhs=w_codes[:, g, :].bitcast(FP8X4),
                rhs_scale=w_scales[:, g, :],
                start=(g == 0),
                stop=(g == PASSES - 1),
            )

        for m in range(2):
            multiply(m, 0)
        for m in range(ROW_TILES):
            if m >= 2:
                multiply(m, 0)
            multiply(m, 1)
            result = results.tile([P, D_OUT], F32)
            nc.vector.tensor_tensor(out=result[:], in0=accs[m][:], in1=bias_all[:], op=ALU.add)
            nc.sync.dma_start(out=out_rows[m * P : (m + 1) * P, :], in_=result[:])
